import numpy as np
import ml_dtypes

BF16 = ml_dtypes.bfloat16


def bf(x):
    return np.asarray(x, np.float32).astype(BF16)


def f32(x):
    return np.asarray(x, np.float32)


def f64(x):
    return np.asarray(x).astype(np.float64)


def striped(idx):
    return np.tile(idx.reshape(-1, 16).T, (8, 1))


C, S, B, BAG, P, M, K, N = 256, 1024, 256, 8, 2, 128, 4, 4096


def crelu(v):
    return np.minimum(np.maximum(v, 0.0), 1.0)


def setup_inputs():
    return {"table": f32(0.3 * np.random.standard_normal((C, S))), "w1": bf(1.5 * np.random.standard_normal((P * C, M)) / np.sqrt(P * C)), "b1": f32(0.2 * np.random.standard_normal((M, 1))), "w2": bf(1.5 * np.random.standard_normal((M, M)) / np.sqrt(M)), "b2": f32(0.2 * np.random.standard_normal((M, 1))), "offs": striped(np.concatenate([np.random.permutation(S) for _ in range(K)]))}


def reference(table, w1, b1, w2, b2, offs):
    idx = offs[:16].T.reshape(-1)
    acc = f64(table)[:, idx].reshape(C, P, BAG, B).sum(axis=2)
    h0 = crelu(acc).transpose(1, 0, 2).reshape(P * C, B)
    h1 = crelu(f64(w1).T @ h0 + f64(b1))
    return crelu(f64(w2).T @ h1 + f64(b2))

@@ -1,0 +1,82 @@
+import concourse.mybir as mybir
+
+F32 = mybir.dt.float32
+BF16 = mybir.dt.bfloat16
+U16 = mybir.dt.uint16
+ADD = mybir.AluOpType.add
+MAX = mybir.AluOpType.max
+MIN = mybir.AluOpType.min
+
+PARTITIONS = 128
+CHANNELS = 256
+FEATURES = 1024
+POSITIONS = 256
+BAG = 8
+SIDES = 2
+HIDDEN = 128
+CHANNEL_BLOCKS = CHANNELS // PARTITIONS
+OFFSETS_PER_COLUMN = 16
+TERM_COLUMNS = POSITIONS // OFFSETS_PER_COLUMN
+
+FLOPS = 2 * SIDES * CHANNELS * HIDDEN * POSITIONS + 2 * HIDDEN * HIDDEN * POSITIONS
+
+
+def tile_nnue_kernel(tc, table, w1, b1, w2, b2, offs, out):
+    nc = tc.nc
+    with (
+        tc.tile_pool(name="held", bufs=1) as held,
+        tc.tile_pool(name="work", bufs=2) as work,
+        tc.psum_pool(name="psum", bufs=1) as psum,
+    ):
+        offsets = held.tile([PARTITIONS, SIDES * BAG * TERM_COLUMNS], U16, name="offsets")
+        nc.sync.dma_start(offsets[:], offs)
+        table_blocks = []
+        for cb in range(CHANNEL_BLOCKS):
+            block = held.tile([PARTITIONS, FEATURES], F32, name=f"table{cb}")
+            nc.scalar.dma_start(block[:], table[cb * PARTITIONS : (cb + 1) * PARTITIONS, :])
+            table_blocks.append(block)
+        w1_sb = held.tile([PARTITIONS, SIDES * CHANNEL_BLOCKS, HIDDEN], BF16, name="w1_sb")
+        nc.sync.dma_start(w1_sb[:], w1.rearrange("(k r) m -> r k m", r=PARTITIONS))
+        w2_sb = held.tile([HIDDEN, HIDDEN], BF16, name="w2_sb")
+        nc.sync.dma_start(w2_sb[:], w2)
+        b1_sb = held.tile([HIDDEN, 1], F32, name="b1_sb")
+        nc.sync.dma_start(b1_sb[:], b1)
+        b2_sb = held.tile([HIDDEN, 1], F32, name="b2_sb")
+        nc.sync.dma_start(b2_sb[:], b2)
+        zeros = held.tile([PARTITIONS, POSITIONS], F32, name="zeros")
+        nc.vector.memset(zeros[:], 0.0)
+
+        layer1 = psum.tile([HIDDEN, POSITIONS], F32, name="layer1")
+        blocks_done = 0
+        for cb in range(CHANNEL_BLOCKS):
+            for p in range(SIDES):
+                bag = zeros
+                for t in range(BAG):
+                    first = (BAG * p + t) * TERM_COLUMNS
+                    picked = table_blocks[cb][:].indirect(offsets[:, first : first + TERM_COLUMNS])
+                    longer_bag = work.tile([PARTITIONS, POSITIONS], F32, name="bag")
+                    nc.vector.tensor_tensor(longer_bag[:], picked, bag[:], ADD)
+                    bag = longer_bag
+                h0 = work.tile([PARTITIONS, POSITIONS], BF16, name="h0")
+                nc.vector.tensor_scalar(h0[:], bag[:], 0.0, 1.0, MAX, MIN)
+                blocks_done += 1
+                nc.tensor.matmul(
+                    layer1[:],
+                    w1_sb[:, CHANNEL_BLOCKS * p + cb, :],
+                    h0[:],
+                    start=(blocks_done == 1),
+                    stop=(blocks_done == SIDES * CHANNEL_BLOCKS),
+                )
+
+        relu1 = work.tile([HIDDEN, POSITIONS], F32, name="relu1")
+        nc.vector.tensor_scalar(relu1[:], layer1[:], b1_sb[:, 0:1], 0.0, ADD, MAX)
+        h1 = work.tile([HIDDEN, POSITIONS], BF16, name="h1")
+        nc.vector.tensor_scalar_min(h1[:], relu1[:], 1.0)
+
+        layer2 = psum.tile([HIDDEN, POSITIONS], F32, name="layer2")
+        nc.tensor.matmul(layer2[:], w2_sb[:], h1[:], start=True, stop=True)
+        relu2 = work.tile([HIDDEN, POSITIONS], F32, name="relu2")
+        nc.vector.tensor_scalar(relu2[:], layer2[:], b2_sb[:, 0:1], 0.0, ADD, MAX)
+        result = work.tile([HIDDEN, POSITIONS], F32, name="result")
+        nc.vector.tensor_scalar_min(result[:], relu2[:], 1.0)
+        nc.sync.dma_start(out, result[:])

@@ -26,6 +26,7 @@ def tile_nnue_kernel(tc, table, w1, b1, w2, b2, offs, out):
     with (
         tc.tile_pool(name="held", bufs=1) as held,
         tc.tile_pool(name="work", bufs=2) as work,
+        tc.tile_pool(name="sums", bufs=3) as sums,
         tc.psum_pool(name="psum", bufs=1) as psum,
     ):
         offsets = held.tile([PARTITIONS, SIDES * BAG * TERM_COLUMNS], U16, name="offsets")
@@ -49,14 +50,16 @@ def tile_nnue_kernel(tc, table, w1, b1, w2, b2, offs, out):
         layer1 = psum.tile([HIDDEN, POSITIONS], F32, name="layer1")
         blocks_done = 0
         for cb in range(CHANNEL_BLOCKS):
-            for p in range(SIDES):
-                bag = zeros
-                for t in range(BAG):
+            bags = [zeros for p in range(SIDES)]
+            for t in range(BAG):
+                for p in range(SIDES):
                     first = (BAG * p + t) * TERM_COLUMNS
                     picked = table_blocks[cb][:].indirect(offsets[:, first : first + TERM_COLUMNS])
-                    longer_bag = work.tile([PARTITIONS, POSITIONS], F32, name="bag")
-                    nc.vector.tensor_tensor(longer_bag[:], picked, bag[:], ADD)
-                    bag = longer_bag
+                    longer_bag = sums.tile([PARTITIONS, POSITIONS], F32, name=f"bag{p}")
+                    nc.vector.tensor_tensor(longer_bag[:], picked, bags[p][:], ADD)
+                    bags[p] = longer_bag
+            for p in range(SIDES):
+                bag = bags[p]
                 h0 = work.tile([PARTITIONS, POSITIONS], BF16, name="h0")
                 nc.vector.tensor_scalar(h0[:], bag[:], 0.0, 1.0, MAX, MIN)
                 blocks_done += 1

@@ -40,14 +40,20 @@ def tile_nnue_kernel(tc, table, w1, b1, w2, b2, offs, out):
         nc.sync.dma_start(w1_sb[:], w1.rearrange("(k r) m -> r k m", r=PARTITIONS))
         w2_sb = held.tile([HIDDEN, HIDDEN], BF16, name="w2_sb")
         nc.sync.dma_start(w2_sb[:], w2)
-        b1_sb = held.tile([HIDDEN, 1], F32, name="b1_sb")
-        nc.sync.dma_start(b1_sb[:], b1)
-        b2_sb = held.tile([HIDDEN, 1], F32, name="b2_sb")
-        nc.sync.dma_start(b2_sb[:], b2)
+        b1_row = held.tile([1, HIDDEN], F32, name="b1_row")
+        nc.sync.dma_start(b1_row[:], b1.rearrange("m one -> one m"))
+        b2_row = held.tile([1, HIDDEN], F32, name="b2_row")
+        nc.sync.dma_start(b2_row[:], b2.rearrange("m one -> one m"))
         zeros = held.tile([PARTITIONS, POSITIONS], F32, name="zeros")
         nc.vector.memset(zeros[:], 0.0)
+        ones_row = held.tile([1, POSITIONS], F32, name="ones_row")
+        nc.vector.memset(ones_row[:], 1.0)
 
         layer1 = psum.tile([HIDDEN, POSITIONS], F32, name="layer1")
+        nc.tensor.matmul(layer1[:], b1_row[:], ones_row[:], start=True, stop=False)
+        layer2 = psum.tile([HIDDEN, POSITIONS], F32, name="layer2")
+        nc.tensor.matmul(layer2[:], b2_row[:], ones_row[:], start=True, stop=False)
+
         blocks_done = 0
         for cb in range(CHANNEL_BLOCKS):
             bags = [zeros for p in range(SIDES)]
@@ -67,19 +73,14 @@ def tile_nnue_kernel(tc, table, w1, b1, w2, b2, offs, out):
                     layer1[:],
                     w1_sb[:, CHANNEL_BLOCKS * p + cb, :],
                     h0[:],
-                    start=(blocks_done == 1),
+                    start=False,
                     stop=(blocks_done == SIDES * CHANNEL_BLOCKS),
                 )
 
-        relu1 = work.tile([HIDDEN, POSITIONS], F32, name="relu1")
-        nc.vector.tensor_scalar(relu1[:], layer1[:], b1_sb[:, 0:1], 0.0, ADD, MAX)
         h1 = work.tile([HIDDEN, POSITIONS], BF16, name="h1")
-        nc.vector.tensor_scalar_min(h1[:], relu1[:], 1.0)
+        nc.vector.tensor_scalar(h1[:], layer1[:], 0.0, 1.0, MAX, MIN)
 
-        layer2 = psum.tile([HIDDEN, POSITIONS], F32, name="layer2")
-        nc.tensor.matmul(layer2[:], w2_sb[:], h1[:], start=True, stop=True)
-        relu2 = work.tile([HIDDEN, POSITIONS], F32, name="relu2")
-        nc.vector.tensor_scalar(relu2[:], layer2[:], b2_sb[:, 0:1], 0.0, ADD, MAX)
+        nc.tensor.matmul(layer2[:], w2_sb[:], h1[:], start=False, stop=True)
         result = work.tile([HIDDEN, POSITIONS], F32, name="result")
-        nc.vector.tensor_scalar_min(result[:], relu2[:], 1.0)
+        nc.vector.tensor_scalar(result[:], layer2[:], 0.0, 1.0, MAX, MIN)
         nc.sync.dma_start(out, result[:])

@@ -17,6 +17,8 @@ HIDDEN = 128
 CHANNEL_BLOCKS = CHANNELS // PARTITIONS
 OFFSETS_PER_COLUMN = 16
 TERM_COLUMNS = POSITIONS // OFFSETS_PER_COLUMN
+HALVES = 2
+HALF = POSITIONS // HALVES
 
 FLOPS = 2 * SIDES * CHANNELS * HIDDEN * POSITIONS + 2 * HIDDEN * HIDDEN * POSITIONS
 
@@ -46,13 +48,14 @@ def tile_nnue_kernel(tc, table, w1, b1, w2, b2, offs, out):
         nc.sync.dma_start(b2_row[:], b2.rearrange("m one -> one m"))
         zeros = held.tile([PARTITIONS, POSITIONS], F32, name="zeros")
         nc.vector.memset(zeros[:], 0.0)
-        ones_row = held.tile([1, POSITIONS], F32, name="ones_row")
+        ones_row = held.tile([1, HALF], F32, name="ones_row")
         nc.vector.memset(ones_row[:], 1.0)
 
-        layer1 = psum.tile([HIDDEN, POSITIONS], F32, name="layer1")
-        nc.tensor.matmul(layer1[:], b1_row[:], ones_row[:], start=True, stop=False)
-        layer2 = psum.tile([HIDDEN, POSITIONS], F32, name="layer2")
-        nc.tensor.matmul(layer2[:], b2_row[:], ones_row[:], start=True, stop=False)
+        layer1 = [psum.tile([HIDDEN, HALF], F32, name=f"layer1_{half}") for half in range(HALVES)]
+        layer2 = [psum.tile([HIDDEN, HALF], F32, name=f"layer2_{half}") for half in range(HALVES)]
+        for half in range(HALVES):
+            nc.tensor.matmul(layer1[half][:], b1_row[:], ones_row[:], start=True, stop=False)
+            nc.tensor.matmul(layer2[half][:], b2_row[:], ones_row[:], start=True, stop=False)
 
         blocks_done = 0
         for cb in range(CHANNEL_BLOCKS):
@@ -69,18 +72,22 @@ def tile_nnue_kernel(tc, table, w1, b1, w2, b2, offs, out):
                 h0 = work.tile([PARTITIONS, POSITIONS], BF16, name="h0")
                 nc.vector.tensor_scalar(h0[:], bag[:], 0.0, 1.0, MAX, MIN)
                 blocks_done += 1
-                nc.tensor.matmul(
-                    layer1[:],
-                    w1_sb[:, CHANNEL_BLOCKS * p + cb, :],
-                    h0[:],
-                    start=False,
-                    stop=(blocks_done == SIDES * CHANNEL_BLOCKS),
-                )
+                for half in range(HALVES):
+                    nc.tensor.matmul(
+                        layer1[half][:],
+                        w1_sb[:, CHANNEL_BLOCKS * p + cb, :],
+                        h0[:, half * HALF : (half + 1) * HALF],
+                        start=False,
+                        stop=(blocks_done == SIDES * CHANNEL_BLOCKS),
+                    )
 
-        h1 = work.tile([HIDDEN, POSITIONS], BF16, name="h1")
-        nc.vector.tensor_scalar(h1[:], layer1[:], 0.0, 1.0, MAX, MIN)
+        h1 = [work.tile([HIDDEN, HALF], BF16, name=f"h1_{half}") for half in range(HALVES)]
+        for half in range(HALVES):
+            nc.vector.tensor_scalar(h1[half][:], layer1[half][:], 0.0, 1.0, MAX, MIN)
 
-        nc.tensor.matmul(layer2[:], w2_sb[:], h1[:], start=False, stop=True)
-        result = work.tile([HIDDEN, POSITIONS], F32, name="result")
-        nc.vector.tensor_scalar(result[:], layer2[:], 0.0, 1.0, MAX, MIN)
-        nc.sync.dma_start(out, result[:])
+        for half in range(HALVES):
+            nc.tensor.matmul(layer2[half][:], w2_sb[:], h1[half][:], start=False, stop=True)
+        for half in range(HALVES):
+            result = work.tile([HIDDEN, HALF], F32, name="result")
+            nc.vector.tensor_scalar(result[:], layer2[half][:], 0.0, 1.0, MAX, MIN)
+            nc.sync.dma_start(out[:, half * HALF : (half + 1) * HALF], result[:])

@@ -6,6 +6,7 @@ U16 = mybir.dt.uint16
 ADD = mybir.AluOpType.add
 MAX = mybir.AluOpType.max
 MIN = mybir.AluOpType.min
+RELU = mybir.ActivationFunctionType.Relu
 
 PARTITIONS = 128
 CHANNELS = 256
@@ -70,7 +71,12 @@ def tile_nnue_kernel(tc, table, w1, b1, w2, b2, offs, out):
             for p in range(SIDES):
                 bag = bags[p]
                 h0 = work.tile([PARTITIONS, POSITIONS], BF16, name="h0")
-                nc.vector.tensor_scalar(h0[:], bag[:], 0.0, 1.0, MAX, MIN)
+                if cb < CHANNEL_BLOCKS - 1:
+                    room = work.tile([PARTITIONS, POSITIONS], F32, name="room")
+                    nc.scalar.activation(room[:], bag[:], RELU, bias=1.0, scale=-1.0)
+                    nc.scalar.activation(h0[:], room[:], RELU, bias=1.0, scale=-1.0)
+                else:
+                    nc.vector.tensor_scalar(h0[:], bag[:], 0.0, 1.0, MAX, MIN)
                 blocks_done += 1
                 for half in range(HALVES):
                     nc.tensor.matmul(

@@ -1,4 +1,5 @@
 import concourse.mybir as mybir
+from concourse.masks import make_identity
 
 F32 = mybir.dt.float32
 BF16 = mybir.dt.bfloat16
@@ -18,6 +19,7 @@ HIDDEN = 128
 CHANNEL_BLOCKS = CHANNELS // PARTITIONS
 OFFSETS_PER_COLUMN = 16
 TERM_COLUMNS = POSITIONS // OFFSETS_PER_COLUMN
+PIECE_TERMS = 4
 HALVES = 2
 HALF = POSITIONS // HALVES
 
@@ -47,8 +49,10 @@ def tile_nnue_kernel(tc, table, w1, b1, w2, b2, offs, out):
         nc.sync.dma_start(b1_row[:], b1.rearrange("m one -> one m"))
         b2_row = held.tile([1, HIDDEN], F32, name="b2_row")
         nc.sync.dma_start(b2_row[:], b2.rearrange("m one -> one m"))
-        zeros = held.tile([PARTITIONS, POSITIONS], F32, name="zeros")
+        zeros = held.tile([PARTITIONS, PIECE_TERMS * POSITIONS], F32, name="zeros")
         nc.vector.memset(zeros[:], 0.0)
+        identity = held.tile([PARTITIONS, PARTITIONS], F32, name="identity")
+        make_identity(nc, identity[:])
         ones_row = held.tile([1, HALF], F32, name="ones_row")
         nc.vector.memset(ones_row[:], 1.0)
 
@@ -60,23 +64,33 @@ def tile_nnue_kernel(tc, table, w1, b1, w2, b2, offs, out):
 
         blocks_done = 0
         for cb in range(CHANNEL_BLOCKS):
-            bags = [zeros for p in range(SIDES)]
-            for t in range(BAG):
+            last_block = cb == CHANNEL_BLOCKS - 1
+            lanes = 1 if last_block else PIECE_TERMS
+            bags = [zeros[:, : lanes * POSITIONS] for p in range(SIDES)]
+            for t in range(0, BAG, lanes):
                 for p in range(SIDES):
                     first = (BAG * p + t) * TERM_COLUMNS
-                    picked = table_blocks[cb][:].indirect(offsets[:, first : first + TERM_COLUMNS])
-                    longer_bag = sums.tile([PARTITIONS, POSITIONS], F32, name=f"bag{p}")
-                    nc.vector.tensor_tensor(longer_bag[:], picked, bags[p][:], ADD)
-                    bags[p] = longer_bag
+                    picked = table_blocks[cb][:].indirect(offsets[:, first : first + lanes * TERM_COLUMNS])
+                    longer_bag = sums.tile([PARTITIONS, lanes * POSITIONS], F32, name=f"bag{p}_{lanes}")
+                    nc.vector.tensor_tensor(longer_bag[:], picked, bags[p], ADD)
+                    bags[p] = longer_bag[:]
             for p in range(SIDES):
-                bag = bags[p]
                 h0 = work.tile([PARTITIONS, POSITIONS], BF16, name="h0")
-                if cb < CHANNEL_BLOCKS - 1:
-                    room = work.tile([PARTITIONS, POSITIONS], F32, name="room")
-                    nc.scalar.activation(room[:], bag[:], RELU, bias=1.0, scale=-1.0)
-                    nc.scalar.activation(h0[:], room[:], RELU, bias=1.0, scale=-1.0)
+                if last_block:
+                    nc.vector.tensor_scalar(h0[:], bags[p], 0.0, 1.0, MAX, MIN)
                 else:
-                    nc.vector.tensor_scalar(h0[:], bag[:], 0.0, 1.0, MAX, MIN)
+                    whole_bag = psum.tile([PARTITIONS, POSITIONS], F32, name=f"whole_bag{p}")
+                    for lane in range(lanes):
+                        nc.tensor.matmul(
+                            whole_bag[:],
+                            identity[:],
+                            bags[p][:, lane * POSITIONS : (lane + 1) * POSITIONS],
+                            start=(lane == 0),
+                            stop=(lane == lanes - 1),
+                        )
+                    room = work.tile([PARTITIONS, POSITIONS], F32, name="room")
+                    nc.scalar.activation(room[:], whole_bag[:], RELU, bias=1.0, scale=-1.0)
+                    nc.scalar.activation(h0[:], room[:], RELU, bias=1.0, scale=-1.0)
                 blocks_done += 1
                 for half in range(HALVES):
                     nc.tensor.matmul(

@@ -17,6 +17,7 @@ BAG = 8
 SIDES = 2
 HIDDEN = 128
 CHANNEL_BLOCKS = CHANNELS // PARTITIONS
+LAST_BLOCK = CHANNEL_BLOCKS - 1
 OFFSETS_PER_COLUMN = 16
 TERM_COLUMNS = POSITIONS // OFFSETS_PER_COLUMN
 PIECE_TERMS = 4
@@ -62,44 +63,60 @@ def tile_nnue_kernel(tc, table, w1, b1, w2, b2, offs, out):
             nc.tensor.matmul(layer1[half][:], b1_row[:], ones_row[:], start=True, stop=False)
             nc.tensor.matmul(layer2[half][:], b2_row[:], ones_row[:], start=True, stop=False)
 
-        blocks_done = 0
+        def gathering_add(cb, p, first_term, terms, onto, name):
+            first = (BAG * p + first_term) * TERM_COLUMNS
+            picked = table_blocks[cb][:].indirect(offsets[:, first : first + terms * TERM_COLUMNS])
+            longer_bag = sums.tile([PARTITIONS, terms * POSITIONS], F32, name=name)
+            nc.vector.tensor_tensor(longer_bag[:], picked, onto, ADD)
+            return longer_bag[:]
+
+        def joined(partial_bags, p):
+            whole_bag = psum.tile([PARTITIONS, POSITIONS], F32, name=f"whole_bag{p}")
+            for lane in range(PIECE_TERMS):
+                nc.tensor.matmul(
+                    whole_bag[:],
+                    identity[:],
+                    partial_bags[:, lane * POSITIONS : (lane + 1) * POSITIONS],
+                    start=(lane == 0),
+                    stop=(lane == PIECE_TERMS - 1),
+                )
+            return whole_bag
+
+        def layer1_add(cb, p, h0, last):
+            for half in range(HALVES):
+                nc.tensor.matmul(
+                    layer1[half][:],
+                    w1_sb[:, CHANNEL_BLOCKS * p + cb, :],
+                    h0[:, half * HALF : (half + 1) * HALF],
+                    start=False,
+                    stop=last,
+                )
+
+        partial = {}
         for cb in range(CHANNEL_BLOCKS):
-            last_block = cb == CHANNEL_BLOCKS - 1
-            lanes = 1 if last_block else PIECE_TERMS
-            bags = [zeros[:, : lanes * POSITIONS] for p in range(SIDES)]
-            for t in range(0, BAG, lanes):
-                for p in range(SIDES):
-                    first = (BAG * p + t) * TERM_COLUMNS
-                    picked = table_blocks[cb][:].indirect(offsets[:, first : first + lanes * TERM_COLUMNS])
-                    longer_bag = sums.tile([PARTITIONS, lanes * POSITIONS], F32, name=f"bag{p}_{lanes}")
-                    nc.vector.tensor_tensor(longer_bag[:], picked, bags[p], ADD)
-                    bags[p] = longer_bag[:]
             for p in range(SIDES):
+                partial[cb, p] = gathering_add(cb, p, 0, PIECE_TERMS, zeros[:], f"first{cb}{p}")
+        bags = []
+        for p in range(SIDES):
+            bag = work.tile([PARTITIONS, POSITIONS], F32, name=f"bag{p}")
+            nc.scalar.copy(bag[:], joined(partial[LAST_BLOCK, p], p)[:])
+            bags.append(bag[:])
+        for cb in range(LAST_BLOCK):
+            for p in range(SIDES):
+                partial[cb, p] = gathering_add(cb, p, PIECE_TERMS, PIECE_TERMS, partial[cb, p], f"second{p}")
+            for p in range(SIDES):
+                room = work.tile([PARTITIONS, POSITIONS], F32, name="room")
+                nc.scalar.activation(room[:], joined(partial[cb, p], p)[:], RELU, bias=1.0, scale=-1.0)
                 h0 = work.tile([PARTITIONS, POSITIONS], BF16, name="h0")
-                if last_block:
-                    nc.vector.tensor_scalar(h0[:], bags[p], 0.0, 1.0, MAX, MIN)
-                else:
-                    whole_bag = psum.tile([PARTITIONS, POSITIONS], F32, name=f"whole_bag{p}")
-                    for lane in range(lanes):
-                        nc.tensor.matmul(
-                            whole_bag[:],
-                            identity[:],
-                            bags[p][:, lane * POSITIONS : (lane + 1) * POSITIONS],
-                            start=(lane == 0),
-                            stop=(lane == lanes - 1),
-                        )
-                    room = work.tile([PARTITIONS, POSITIONS], F32, name="room")
-                    nc.scalar.activation(room[:], whole_bag[:], RELU, bias=1.0, scale=-1.0)
-                    nc.scalar.activation(h0[:], room[:], RELU, bias=1.0, scale=-1.0)
-                blocks_done += 1
-                for half in range(HALVES):
-                    nc.tensor.matmul(
-                        layer1[half][:],
-                        w1_sb[:, CHANNEL_BLOCKS * p + cb, :],
-                        h0[:, half * HALF : (half + 1) * HALF],
-                        start=False,
-                        stop=(blocks_done == SIDES * CHANNEL_BLOCKS),
-                    )
+                nc.scalar.activation(h0[:], room[:], RELU, bias=1.0, scale=-1.0)
+                layer1_add(cb, p, h0, False)
+        for t in range(PIECE_TERMS, BAG):
+            for p in range(SIDES):
+                bags[p] = gathering_add(LAST_BLOCK, p, t, 1, bags[p], f"chain{p}")
+        for p in range(SIDES):
+            h0 = work.tile([PARTITIONS, POSITIONS], BF16, name="h0")
+            nc.vector.tensor_scalar(h0[:], bags[p], 0.0, 1.0, MAX, MIN)
+            layer1_add(LAST_BLOCK, p, h0, p == SIDES - 1)
 
         h1 = [work.tile([HIDDEN, HALF], BF16, name=f"h1_{half}") for half in range(HALVES)]
         for half in range(HALVES):

@@ -17,7 +17,8 @@ BAG = 8
 SIDES = 2
 HIDDEN = 128
 CHANNEL_BLOCKS = CHANNELS // PARTITIONS
-LAST_BLOCK = CHANNEL_BLOCKS - 1
+LAST_BLOCK = 0
+OTHER_BLOCKS = range(1, CHANNEL_BLOCKS)
 OFFSETS_PER_COLUMN = 16
 TERM_COLUMNS = POSITIONS // OFFSETS_PER_COLUMN
 PIECE_TERMS = 4
@@ -101,7 +102,7 @@ def tile_nnue_kernel(tc, table, w1, b1, w2, b2, offs, out):
             bag = work.tile([PARTITIONS, POSITIONS], F32, name=f"bag{p}")
             nc.scalar.copy(bag[:], joined(partial[LAST_BLOCK, p], p)[:])
             bags.append(bag[:])
-        for cb in range(LAST_BLOCK):
+        for cb in OTHER_BLOCKS:
             for p in range(SIDES):
                 partial[cb, p] = gathering_add(cb, p, PIECE_TERMS, PIECE_TERMS, partial[cb, p], f"second{p}")
             for p in range(SIDES):
@@ -110,13 +111,30 @@ def tile_nnue_kernel(tc, table, w1, b1, w2, b2, offs, out):
                 h0 = work.tile([PARTITIONS, POSITIONS], BF16, name="h0")
                 nc.scalar.activation(h0[:], room[:], RELU, bias=1.0, scale=-1.0)
                 layer1_add(cb, p, h0, False)
-        for t in range(PIECE_TERMS, BAG):
+        for t in range(PIECE_TERMS, BAG - 1):
             for p in range(SIDES):
                 bags[p] = gathering_add(LAST_BLOCK, p, t, 1, bags[p], f"chain{p}")
-        for p in range(SIDES):
-            h0 = work.tile([PARTITIONS, POSITIONS], BF16, name="h0")
-            nc.vector.tensor_scalar(h0[:], bags[p], 0.0, 1.0, MAX, MIN)
-            layer1_add(LAST_BLOCK, p, h0, p == SIDES - 1)
+        HALF_COLUMNS = TERM_COLUMNS // HALVES
+        whole = {}
+        for half in range(HALVES):
+            for p in range(SIDES):
+                first = (BAG * p + BAG - 1) * TERM_COLUMNS + half * HALF_COLUMNS
+                picked = table_blocks[LAST_BLOCK][:].indirect(offsets[:, first : first + HALF_COLUMNS])
+                whole[p, half] = sums.tile([PARTITIONS, HALF], F32, name=f"whole{p}{half}")
+                nc.vector.tensor_tensor(
+                    whole[p, half][:], picked, bags[p][:, half * HALF : (half + 1) * HALF], ADD
+                )
+        for half in range(HALVES):
+            for p in range(SIDES):
+                h0 = work.tile([PARTITIONS, HALF], BF16, name=f"h0_half{p}")
+                nc.vector.tensor_scalar(h0[:], whole[p, half][:], 0.0, 1.0, MAX, MIN)
+                nc.tensor.matmul(
+                    layer1[half][:],
+                    w1_sb[:, CHANNEL_BLOCKS * p + LAST_BLOCK, :],
+                    h0[:],
+                    start=False,
+                    stop=(p == SIDES - 1),
+                )
 
         h1 = [work.tile([HIDDEN, HALF], BF16, name=f"h1_{half}") for half in range(HALVES)]
         for half in range(HALVES):

@@ -41,10 +41,10 @@ def tile_nnue_kernel(tc, table, w1, b1, w2, b2, offs, out):
         table_blocks = []
         for cb in range(CHANNEL_BLOCKS):
             block = held.tile([PARTITIONS, FEATURES], F32, name=f"table{cb}")
-            nc.scalar.dma_start(block[:], table[cb * PARTITIONS : (cb + 1) * PARTITIONS, :])
+            nc.scalar.dma_start(block[:], table[cb::CHANNEL_BLOCKS, :])
             table_blocks.append(block)
-        w1_sb = held.tile([PARTITIONS, SIDES * CHANNEL_BLOCKS, HIDDEN], BF16, name="w1_sb")
-        nc.sync.dma_start(w1_sb[:], w1.rearrange("(k r) m -> r k m", r=PARTITIONS))
+        w1_sb = held.tile([PARTITIONS, SIDES, CHANNEL_BLOCKS, HIDDEN], BF16, name="w1_sb")
+        nc.sync.dma_start(w1_sb[:], w1.rearrange("(p r cb) m -> r p cb m", p=SIDES, cb=CHANNEL_BLOCKS))
         w2_sb = held.tile([HIDDEN, HIDDEN], BF16, name="w2_sb")
         nc.sync.dma_start(w2_sb[:], w2)
         b1_row = held.tile([1, HIDDEN], F32, name="b1_row")
@@ -87,7 +87,7 @@ def tile_nnue_kernel(tc, table, w1, b1, w2, b2, offs, out):
             for half in range(HALVES):
                 nc.tensor.matmul(
                     layer1[half][:],
-                    w1_sb[:, CHANNEL_BLOCKS * p + cb, :],
+                    w1_sb[:, p, cb, :],
                     h0[:, half * HALF : (half + 1) * HALF],
                     start=False,
                     stop=last,
@@ -130,7 +130,7 @@ def tile_nnue_kernel(tc, table, w1, b1, w2, b2, offs, out):
                 nc.vector.tensor_scalar(h0[:], whole[p, half][:], 0.0, 1.0, MAX, MIN)
                 nc.tensor.matmul(
                     layer1[half][:],
-                    w1_sb[:, CHANNEL_BLOCKS * p + LAST_BLOCK, :],
+                    w1_sb[:, p, LAST_BLOCK, :],
                     h0[:],
                     start=False,
                     stop=(p == SIDES - 1),

@@ -145,4 +145,5 @@ def tile_nnue_kernel(tc, table, w1, b1, w2, b2, offs, out):
         for half in range(HALVES):
             result = work.tile([HIDDEN, HALF], F32, name="result")
             nc.vector.tensor_scalar(result[:], layer2[half][:], 0.0, 1.0, MAX, MIN)
-            nc.sync.dma_start(out[:, half * HALF : (half + 1) * HALF], result[:])
+            store_queue = nc.sync if half == 0 else nc.scalar
+            store_queue.dma_start(out[:, half * HALF : (half + 1) * HALF], result[:])

@@ -24,6 +24,7 @@ TERM_COLUMNS = POSITIONS // OFFSETS_PER_COLUMN
 PIECE_TERMS = 4
 HALVES = 2
 HALF = POSITIONS // HALVES
+FIRST_SIDE, LAST_SIDE = range(SIDES)
 
 FLOPS = 2 * SIDES * CHANNELS * HIDDEN * POSITIONS + 2 * HIDDEN * HIDDEN * POSITIONS
 
@@ -114,26 +115,33 @@ def tile_nnue_kernel(tc, table, w1, b1, w2, b2, offs, out):
         for t in range(PIECE_TERMS, BAG - 1):
             for p in range(SIDES):
                 bags[p] = gathering_add(LAST_BLOCK, p, t, 1, bags[p], f"chain{p}")
-        HALF_COLUMNS = TERM_COLUMNS // HALVES
-        whole = {}
+        ready = sums.tile([PARTITIONS, POSITIONS + HALF], F32, name="ready")
+        late = sums.tile([PARTITIONS, HALF], F32, name="late")
+
+        def add_last_term(p, first_position, positions, whole):
+            first = (BAG * p + BAG - 1) * TERM_COLUMNS + first_position // OFFSETS_PER_COLUMN
+            picked = table_blocks[LAST_BLOCK][:].indirect(offsets[:, first : first + positions // OFFSETS_PER_COLUMN])
+            nc.vector.tensor_tensor(whole, picked, bags[p][:, first_position : first_position + positions], ADD)
+
+        add_last_term(FIRST_SIDE, 0, POSITIONS, ready[:, :POSITIONS])
+        add_last_term(LAST_SIDE, 0, HALF, ready[:, POSITIONS:])
+        add_last_term(LAST_SIDE, HALF, HALF, late[:])
+        h0_ready = work.tile([PARTITIONS, POSITIONS + HALF], BF16, name="h0_ready")
+        nc.vector.tensor_scalar(h0_ready[:], ready[:], 0.0, 1.0, MAX, MIN)
+        h0_late = work.tile([PARTITIONS, HALF], BF16, name="h0_late")
+        nc.vector.tensor_scalar(h0_late[:], late[:], 0.0, 1.0, MAX, MIN)
+        h0_parts = [
+            [h0_ready[:, :HALF], h0_ready[:, POSITIONS:]],
+            [h0_ready[:, HALF:POSITIONS], h0_late[:]],
+        ]
         for half in range(HALVES):
             for p in range(SIDES):
-                first = (BAG * p + BAG - 1) * TERM_COLUMNS + half * HALF_COLUMNS
-                picked = table_blocks[LAST_BLOCK][:].indirect(offsets[:, first : first + HALF_COLUMNS])
-                whole[p, half] = sums.tile([PARTITIONS, HALF], F32, name=f"whole{p}{half}")
-                nc.vector.tensor_tensor(
-                    whole[p, half][:], picked, bags[p][:, half * HALF : (half + 1) * HALF], ADD
-                )
-        for half in range(HALVES):
-            for p in range(SIDES):
-                h0 = work.tile([PARTITIONS, HALF], BF16, name=f"h0_half{p}")
-                nc.vector.tensor_scalar(h0[:], whole[p, half][:], 0.0, 1.0, MAX, MIN)
                 nc.tensor.matmul(
                     layer1[half][:],
                     w1_sb[:, p, LAST_BLOCK, :],
-                    h0[:],
+                    h0_parts[half][p],
                     start=False,
-                    stop=(p == SIDES - 1),
+                    stop=(p == LAST_SIDE),
                 )
 
         h1 = [work.tile([HIDDEN, HALF], BF16, name=f"h1_{half}") for half in range(HALVES)]

@@ -115,34 +115,25 @@ def tile_nnue_kernel(tc, table, w1, b1, w2, b2, offs, out):
         for t in range(PIECE_TERMS, BAG - 1):
             for p in range(SIDES):
                 bags[p] = gathering_add(LAST_BLOCK, p, t, 1, bags[p], f"chain{p}")
-        ready = sums.tile([PARTITIONS, POSITIONS + HALF], F32, name="ready")
-        late = sums.tile([PARTITIONS, HALF], F32, name="late")
-
-        def add_last_term(p, first_position, positions, whole):
+        def add_last_term(p, first_position, positions):
             first = (BAG * p + BAG - 1) * TERM_COLUMNS + first_position // OFFSETS_PER_COLUMN
             picked = table_blocks[LAST_BLOCK][:].indirect(offsets[:, first : first + positions // OFFSETS_PER_COLUMN])
-            nc.vector.tensor_tensor(whole, picked, bags[p][:, first_position : first_position + positions], ADD)
+            whole = sums.tile([PARTITIONS, positions], F32, name=f"whole{p}")
+            nc.vector.tensor_tensor(whole[:], picked, bags[p][:, first_position : first_position + positions], ADD)
+            return whole[:]
 
-        add_last_term(FIRST_SIDE, 0, POSITIONS, ready[:, :POSITIONS])
-        add_last_term(LAST_SIDE, 0, HALF, ready[:, POSITIONS:])
-        add_last_term(LAST_SIDE, HALF, HALF, late[:])
-        h0_ready = work.tile([PARTITIONS, POSITIONS + HALF], BF16, name="h0_ready")
-        nc.vector.tensor_scalar(h0_ready[:], ready[:], 0.0, 1.0, MAX, MIN)
-        h0_late = work.tile([PARTITIONS, HALF], BF16, name="h0_late")
-        nc.vector.tensor_scalar(h0_late[:], late[:], 0.0, 1.0, MAX, MIN)
-        h0_parts = [
-            [h0_ready[:, :HALF], h0_ready[:, POSITIONS:]],
-            [h0_ready[:, HALF:POSITIONS], h0_late[:]],
-        ]
+        def vector_crelu(v, positions):
+            h0 = work.tile([PARTITIONS, positions], BF16, name=f"h0_{positions}")
+            nc.vector.tensor_scalar(h0[:], v, 0.0, 1.0, MAX, MIN)
+            return h0
+
+        first_whole = add_last_term(FIRST_SIDE, 0, POSITIONS)
+        last_whole = [add_last_term(LAST_SIDE, 0, HALF)]
+        layer1_add(LAST_BLOCK, FIRST_SIDE, vector_crelu(first_whole, POSITIONS), False)
+        last_whole.append(add_last_term(LAST_SIDE, HALF, HALF))
         for half in range(HALVES):
-            for p in range(SIDES):
-                nc.tensor.matmul(
-                    layer1[half][:],
-                    w1_sb[:, p, LAST_BLOCK, :],
-                    h0_parts[half][p],
-                    start=False,
-                    stop=(p == LAST_SIDE),
-                )
+            h0 = vector_crelu(last_whole[half], HALF)
+            nc.tensor.matmul(layer1[half][:], w1_sb[:, LAST_SIDE, LAST_BLOCK, :], h0[:], start=False, stop=True)
 
         h1 = [work.tile([HIDDEN, HALF], BF16, name=f"h1_{half}") for half in range(HALVES)]
         for half in range(HALVES):

@@ -115,25 +115,30 @@ def tile_nnue_kernel(tc, table, w1, b1, w2, b2, offs, out):
         for t in range(PIECE_TERMS, BAG - 1):
             for p in range(SIDES):
                 bags[p] = gathering_add(LAST_BLOCK, p, t, 1, bags[p], f"chain{p}")
-        def add_last_term(p, first_position, positions):
+        def add_last_term(p, first_position, positions, whole):
             first = (BAG * p + BAG - 1) * TERM_COLUMNS + first_position // OFFSETS_PER_COLUMN
             picked = table_blocks[LAST_BLOCK][:].indirect(offsets[:, first : first + positions // OFFSETS_PER_COLUMN])
-            whole = sums.tile([PARTITIONS, positions], F32, name=f"whole{p}")
-            nc.vector.tensor_tensor(whole[:], picked, bags[p][:, first_position : first_position + positions], ADD)
-            return whole[:]
+            nc.vector.tensor_tensor(whole, picked, bags[p][:, first_position : first_position + positions], ADD)
 
-        def vector_crelu(v, positions):
-            h0 = work.tile([PARTITIONS, positions], BF16, name=f"h0_{positions}")
+        def vector_crelu(v, name):
+            h0 = work.tile(v.shape, BF16, name=name)
             nc.vector.tensor_scalar(h0[:], v, 0.0, 1.0, MAX, MIN)
             return h0
 
-        first_whole = add_last_term(FIRST_SIDE, 0, POSITIONS)
-        last_whole = [add_last_term(LAST_SIDE, 0, HALF)]
-        layer1_add(LAST_BLOCK, FIRST_SIDE, vector_crelu(first_whole, POSITIONS), False)
-        last_whole.append(add_last_term(LAST_SIDE, HALF, HALF))
+        ready = sums.tile([PARTITIONS, POSITIONS + HALF], F32, name="ready")
+        add_last_term(FIRST_SIDE, 0, POSITIONS, ready[:, :POSITIONS])
+        add_last_term(LAST_SIDE, 0, HALF, ready[:, POSITIONS:])
+        h0_early = vector_crelu(ready[:, :HALF], "h0_early")
+        late = sums.tile([PARTITIONS, HALF], F32, name="late")
+        add_last_term(LAST_SIDE, HALF, HALF, late[:])
+        h0_ready = vector_crelu(ready[:, HALF:], "h0_ready")
+        h0_late = vector_crelu(late[:], "h0_late")
+        h0_parts = [[h0_early[:], h0_ready[:, HALF:]], [h0_ready[:, :HALF], h0_late[:]]]
         for half in range(HALVES):
-            h0 = vector_crelu(last_whole[half], HALF)
-            nc.tensor.matmul(layer1[half][:], w1_sb[:, LAST_SIDE, LAST_BLOCK, :], h0[:], start=False, stop=True)
+            for p in range(SIDES):
+                nc.tensor.matmul(
+                    layer1[half][:], w1_sb[:, p, LAST_BLOCK, :], h0_parts[half][p], start=False, stop=(p == LAST_SIDE)
+                )
 
         h1 = [work.tile([HIDDEN, HALF], BF16, name=f"h1_{half}") for half in range(HALVES)]
         for half in range(HALVES):

@@ -149,5 +149,4 @@ def tile_nnue_kernel(tc, table, w1, b1, w2, b2, offs, out):
         for half in range(HALVES):
             result = work.tile([HIDDEN, HALF], F32, name="result")
             nc.vector.tensor_scalar(result[:], layer2[half][:], 0.0, 1.0, MAX, MIN)
-            store_queue = nc.sync if half == 0 else nc.scalar
-            store_queue.dma_start(out[:, half * HALF : (half + 1) * HALF], result[:])
+            nc.scalar.dma_start(out[:, half * HALF : (half + 1) * HALF], result[:])

@@ -146,7 +146,9 @@ def tile_nnue_kernel(tc, table, w1, b1, w2, b2, offs, out):
 
         for half in range(HALVES):
             nc.tensor.matmul(layer2[half][:], w2_sb[:], h1[half][:], start=False, stop=True)
+        result = work.tile([HIDDEN, POSITIONS], F32, name="result")
         for half in range(HALVES):
-            result = work.tile([HIDDEN, HALF], F32, name="result")
-            nc.vector.tensor_scalar(result[:], layer2[half][:], 0.0, 1.0, MAX, MIN)
-            nc.scalar.dma_start(out[:, half * HALF : (half + 1) * HALF], result[:])
+            nc.vector.tensor_scalar(
+                result[:, half * HALF : (half + 1) * HALF], layer2[half][:], 0.0, 1.0, MAX, MIN
+            )
+        nc.scalar.dma_start(out, result[:])

import concourse.mybir as mybir
from concourse.masks import make_identity

F32 = mybir.dt.float32
BF16 = mybir.dt.bfloat16
U16 = mybir.dt.uint16
ADD = mybir.AluOpType.add
MAX = mybir.AluOpType.max
MIN = mybir.AluOpType.min
RELU = mybir.ActivationFunctionType.Relu

PARTITIONS = 128
CHANNELS = 256
FEATURES = 1024
POSITIONS = 256
BAG = 8
SIDES = 2
HIDDEN = 128
CHANNEL_BLOCKS = CHANNELS // PARTITIONS
LAST_BLOCK = 0
OTHER_BLOCKS = range(1, CHANNEL_BLOCKS)
OFFSETS_PER_COLUMN = 16
TERM_COLUMNS = POSITIONS // OFFSETS_PER_COLUMN
PIECE_TERMS = 4
HALVES = 2
HALF = POSITIONS // HALVES
FIRST_SIDE, LAST_SIDE = range(SIDES)

FLOPS = 2 * SIDES * CHANNELS * HIDDEN * POSITIONS + 2 * HIDDEN * HIDDEN * POSITIONS


def tile_nnue_kernel(tc, table, w1, b1, w2, b2, offs, out):
    nc = tc.nc
    with (
        tc.tile_pool(name="held", bufs=1) as held,
        tc.tile_pool(name="work", bufs=2) as work,
        tc.tile_pool(name="sums", bufs=3) as sums,
        tc.psum_pool(name="psum", bufs=1) as psum,
    ):
        offsets = held.tile([PARTITIONS, SIDES * BAG * TERM_COLUMNS], U16, name="offsets")
        nc.sync.dma_start(offsets[:], offs)
        table_blocks = []
        for cb in range(CHANNEL_BLOCKS):
            block = held.tile([PARTITIONS, FEATURES], F32, name=f"table{cb}")
            nc.scalar.dma_start(block[:], table[cb::CHANNEL_BLOCKS, :])
            table_blocks.append(block)
        w1_sb = held.tile([PARTITIONS, SIDES, CHANNEL_BLOCKS, HIDDEN], BF16, name="w1_sb")
        nc.sync.dma_start(w1_sb[:], w1.rearrange("(p r cb) m -> r p cb m", p=SIDES, cb=CHANNEL_BLOCKS))
        w2_sb = held.tile([HIDDEN, HIDDEN], BF16, name="w2_sb")
        nc.sync.dma_start(w2_sb[:], w2)
        b1_row = held.tile([1, HIDDEN], F32, name="b1_row")
        nc.sync.dma_start(b1_row[:], b1.rearrange("m one -> one m"))
        b2_row = held.tile([1, HIDDEN], F32, name="b2_row")
        nc.sync.dma_start(b2_row[:], b2.rearrange("m one -> one m"))
        zeros = held.tile([PARTITIONS, PIECE_TERMS * POSITIONS], F32, name="zeros")
        nc.vector.memset(zeros[:], 0.0)
        identity = held.tile([PARTITIONS, PARTITIONS], F32, name="identity")
        make_identity(nc, identity[:])
        ones_row = held.tile([1, HALF], F32, name="ones_row")
        nc.vector.memset(ones_row[:], 1.0)

        layer1 = [psum.tile([HIDDEN, HALF], F32, name=f"layer1_{half}") for half in range(HALVES)]
        layer2 = [psum.tile([HIDDEN, HALF], F32, name=f"layer2_{half}") for half in range(HALVES)]
        for half in range(HALVES):
            nc.tensor.matmul(layer1[half][:], b1_row[:], ones_row[:], start=True, stop=False)
            nc.tensor.matmul(layer2[half][:], b2_row[:], ones_row[:], start=True, stop=False)

        def gathering_add(cb, p, first_term, terms, onto, name):
            first = (BAG * p + first_term) * TERM_COLUMNS
            picked = table_blocks[cb][:].indirect(offsets[:, first : first + terms * TERM_COLUMNS])
            longer_bag = sums.tile([PARTITIONS, terms * POSITIONS], F32, name=name)
            nc.vector.tensor_tensor(longer_bag[:], picked, onto, ADD)
            return longer_bag[:]

        def joined(partial_bags, p):
            whole_bag = psum.tile([PARTITIONS, POSITIONS], F32, name=f"whole_bag{p}")
            for lane in range(PIECE_TERMS):
                nc.tensor.matmul(
                    whole_bag[:],
                    identity[:],
                    partial_bags[:, lane * POSITIONS : (lane + 1) * POSITIONS],
                    start=(lane == 0),
                    stop=(lane == PIECE_TERMS - 1),
                )
            return whole_bag

        def layer1_add(cb, p, h0, last):
            for half in range(HALVES):
                nc.tensor.matmul(
                    layer1[half][:],
                    w1_sb[:, p, cb, :],
                    h0[:, half * HALF : (half + 1) * HALF],
                    start=False,
                    stop=last,
                )

        partial = {}
        for cb in range(CHANNEL_BLOCKS):
            for p in range(SIDES):
                partial[cb, p] = gathering_add(cb, p, 0, PIECE_TERMS, zeros[:], f"first{cb}{p}")
        bags = []
        for p in range(SIDES):
            bag = work.tile([PARTITIONS, POSITIONS], F32, name=f"bag{p}")
            nc.scalar.copy(bag[:], joined(partial[LAST_BLOCK, p], p)[:])
            bags.append(bag[:])
        for cb in OTHER_BLOCKS:
            for p in range(SIDES):
                partial[cb, p] = gathering_add(cb, p, PIECE_TERMS, PIECE_TERMS, partial[cb, p], f"second{p}")
            for p in range(SIDES):
                room = work.tile([PARTITIONS, POSITIONS], F32, name="room")
                nc.scalar.activation(room[:], joined(partial[cb, p], p)[:], RELU, bias=1.0, scale=-1.0)
                h0 = work.tile([PARTITIONS, POSITIONS], BF16, name="h0")
                nc.scalar.activation(h0[:], room[:], RELU, bias=1.0, scale=-1.0)
                layer1_add(cb, p, h0, False)
        for t in range(PIECE_TERMS, BAG - 1):
            for p in range(SIDES):
                bags[p] = gathering_add(LAST_BLOCK, p, t, 1, bags[p], f"chain{p}")
        def add_last_term(p, first_position, positions, whole):
            first = (BAG * p + BAG - 1) * TERM_COLUMNS + first_position // OFFSETS_PER_COLUMN
            picked = table_blocks[LAST_BLOCK][:].indirect(offsets[:, first : first + positions // OFFSETS_PER_COLUMN])
            nc.vector.tensor_tensor(whole, picked, bags[p][:, first_position : first_position + positions], ADD)

        def vector_crelu(v, name):
            h0 = work.tile(v.shape, BF16, name=name)
            nc.vector.tensor_scalar(h0[:], v, 0.0, 1.0, MAX, MIN)
            return h0

        ready = sums.tile([PARTITIONS, POSITIONS + HALF], F32, name="ready")
        add_last_term(FIRST_SIDE, 0, POSITIONS, ready[:, :POSITIONS])
        add_last_term(LAST_SIDE, 0, HALF, ready[:, POSITIONS:])
        h0_early = vector_crelu(ready[:, :HALF], "h0_early")
        late = sums.tile([PARTITIONS, HALF], F32, name="late")
        add_last_term(LAST_SIDE, HALF, HALF, late[:])
        h0_ready = vector_crelu(ready[:, HALF:], "h0_ready")
        h0_late = vector_crelu(late[:], "h0_late")
        h0_parts = [[h0_early[:], h0_ready[:, HALF:]], [h0_ready[:, :HALF], h0_late[:]]]
        for half in range(HALVES):
            for p in range(SIDES):
                nc.tensor.matmul(
                    layer1[half][:], w1_sb[:, p, LAST_BLOCK, :], h0_parts[half][p], start=False, stop=(p == LAST_SIDE)
                )

        h1 = [work.tile([HIDDEN, HALF], BF16, name=f"h1_{half}") for half in range(HALVES)]
        for half in range(HALVES):
            nc.vector.tensor_scalar(h1[half][:], layer1[half][:], 0.0, 1.0, MAX, MIN)

        for half in range(HALVES):
            nc.tensor.matmul(layer2[half][:], w2_sb[:], h1[half][:], start=False, stop=True)
        result = work.tile([HIDDEN, POSITIONS], F32, name="result")
        for half in range(HALVES):
            nc.vector.tensor_scalar(
                result[:, half * HALF : (half + 1) * HALF], layer2[half][:], 0.0, 1.0, MAX, MIN
            )
        nc.scalar.dma_start(out, result[:])
